import numpy as np
import ml_dtypes


def mxq(x, axis, fmt="e4m3"):
    dtype, down = {"e4m3": (ml_dtypes.float8_e4m3fn, 7), "e5m2": (ml_dtypes.float8_e5m2, 14)}[fmt]
    v = np.moveaxis(np.asarray(x, np.float32).astype(ml_dtypes.bfloat16).astype(np.float64), axis, -1)
    blocks = v.reshape(v.shape[:-1] + (-1, 32))
    amax = np.abs(blocks).max(-1, keepdims=True)
    byte = np.maximum(np.where(amax > 0, np.frexp(amax)[1] - 1 + 127, 0) - down, 1)
    scale = np.exp2(byte - 127.0)
    codes = (blocks / scale).astype(np.float32).astype(dtype).astype(np.float64)
    return np.moveaxis((codes * scale).reshape(v.shape), -1, axis)


WIDE = False


def mx_kscale(k):
    if not WIDE:
        return np.ones(k)
    levels = np.array([10, -10, 5, -5, 0])
    a = np.random.permutation(np.resize(levels, k // 512 * 4)).reshape(k // 512, 4)
    idx = np.arange(k)
    return np.exp2(a[idx // 512, idx % 128 // 32])


BF16 = ml_dtypes.bfloat16


def bf(x):
    return np.asarray(x, np.float32).astype(BF16)


def f64(x):
    return np.asarray(x).astype(np.float64)


B, C, HD, F, G, O = 128, 8, 8, 1024, 512, 128
N = C * HD


def setup_inputs():
    s, t = mx_kscale(F), mx_kscale(G)
    return {
        "x": bf(np.random.standard_normal((B, C, HD, F)) * s),
        "W1g": bf(np.random.standard_normal((G, F)) * 0.7 * np.sqrt(N / F) / s * t[:, None]),
        "b1g": bf(np.random.standard_normal(G) * 0.2 * t),
        "W2g": bf(np.random.standard_normal((O, G)) * 1.5 / np.sqrt(G) / t),
        "b2g": bf(np.random.standard_normal(O) * 0.2),
    }


def reference(x, W1g, b1g, W2g, b2g):
    xn = f64(x).reshape(B * N, F)
    y = mxq(xn, 1, "e4m3") @ mxq(f64(W1g), 1, "e4m3").T
    m1 = np.maximum(y.reshape(B, N, G).sum(1) / N + f64(b1g), 0.0)
    m2 = np.maximum((mxq(m1, 1, "e4m3") @ mxq(f64(W2g), 1, "e4m3").T) + f64(b2g), 0.0)
    return np.broadcast_to(m2[:, None, :], (B, N, O)).copy()

@@ -1,0 +1,241 @@
+from contextlib import ExitStack
+
+import concourse.mybir as mybir
+from concourse.masks import make_identity
+
+F32 = mybir.dt.float32
+BF16 = mybir.dt.bfloat16
+U32 = mybir.dt.uint32
+U8 = mybir.dt.uint8
+FP8X4 = mybir.dt.float8_e4m3fn_x4
+ALU = mybir.AluOpType
+ACT = mybir.ActivationFunctionType
+AX = mybir.AxisListType
+
+P = 128
+NODES = 64
+FEAT = 1024
+HID = 512
+OUTF = 128
+GROUPS = 4
+UNITS = 16
+SLOTS = 4
+
+FLOPS = 2 * 8192 * FEAT * HID + 2 * 128 * HID * OUTF
+
+VEC_COPIES = [2, 1, 1, 1, 1, 0, 1, 1, 1, 0, 1, 1, 1, 0, 1, 1]
+
+
+def tile_gcn_pa_t_kernel(tc, x, W1g, b1g, W2g, b2g, out):
+    nc = tc.nc
+    ctx = ExitStack()
+    with ctx:
+        const = ctx.enter_context(tc.tile_pool(name="const", bufs=1))
+        xpool = ctx.enter_context(tc.tile_pool(name="xpool", bufs=UNITS))
+        gpool = ctx.enter_context(tc.tile_pool(name="gpool", bufs=2))
+        cpool = ctx.enter_context(tc.tile_pool(name="cpool", bufs=3))
+        epool = ctx.enter_context(tc.tile_pool(name="epool", bufs=2))
+        tpool = ctx.enter_context(tc.psum_pool(name="tpool", bufs=4))
+        apool = ctx.enter_context(tc.psum_pool(name="apool", bufs=1))
+        ctx.enter_context(tc.manual_schedule())
+
+        xv = x.flatten_outer_dims().rearrange("(g q s) f -> g q (s f)", g=GROUPS, q=P)
+        ov = out.flatten_outer_dims().rearrange("(g q s) o -> g q (s o)", g=GROUPS, q=P)
+
+        ident = const.tile([P, P], F32)
+        make_identity(nc, ident[:])
+        warm = const.tile([P, 1], F32)
+        warm2 = const.tile([P, 1], F32)
+        nc.vector.memset(warm[:], 0.0)
+        nc.scalar.activation(out=warm2[:], in_=warm[:], func=ACT.Relu)
+
+        xt = []
+        for i in range(UNITS):
+            x_sb = xpool.tile([P, SLOTS * FEAT], BF16, name="x_sb")
+            xt.append(x_sb)
+        w1raw = const.tile([P, SLOTS * FEAT], BF16)
+        w1v = W1g.rearrange("(p j) k -> p (j k)", j=SLOTS)
+
+        def load_x(i, pieces):
+            g, c = divmod(i, 4)
+            w = SLOTS * FEAT // pieces
+            for s in range(pieces):
+                nc.sync.dma_start(
+                    out=xt[i][:, s * w : (s + 1) * w],
+                    in_=xv[g, :, c * SLOTS * FEAT + s * w : c * SLOTS * FEAT + (s + 1) * w],
+                )
+
+        load_x(0, 4)
+        for j in range(SLOTS):
+            nc.sync.dma_start(out=w1raw[:, j * FEAT : (j + 1) * FEAT], in_=w1v[:, j * FEAT : (j + 1) * FEAT])
+        for i in range(1, UNITS):
+            load_x(i, 1)
+
+        w2raw = const.tile([P, HID], BF16)
+        nc.scalar.dma_start(out=w2raw[:], in_=W2g)
+        b1raw = const.tile([P, SLOTS], BF16)
+        nc.scalar.dma_start(out=b1raw[:], in_=b1g.rearrange("(p j) -> p j", j=SLOTS))
+        b2raw = const.tile([P, OUTF], BF16)
+        nc.scalar.dma_start(out=b2raw[:], in_=b2g.partition_broadcast(P))
+
+        w1grp = const.tile([P, SLOTS * FEAT], BF16, align_bytes=64)
+        w1codes = const.tile([P, SLOTS * FEAT // 4], U32, align_bytes=64)
+        w1scales = const.tile([P, SLOTS * FEAT // 4], U8, align_bytes=64)
+        w2grp = const.tile([P, HID], BF16, align_bytes=64)
+        w2codes = const.tile([P, OUTF], U32, align_bytes=64)
+        w2scales = const.tile([P, OUTF], U8, align_bytes=64)
+        b1f = const.tile([P, SLOTS], F32)
+        b2f = const.tile([P, OUTF], F32)
+
+        state = {}
+
+        def copy_out(engine_is_vector, dst, src):
+            if engine_is_vector:
+                nc.vector.tensor_copy(out=dst, in_=src)
+            else:
+                nc.scalar.copy(out=dst, in_=src)
+
+        def transposes(src_f32, s):
+            bank = tpool.tile([P, 512], F32, name="bank")
+            for v in range(4):
+                nc.tensor.transpose(
+                    bank[:, v * P : (v + 1) * P],
+                    src_f32[:, s * 512 + v * P : s * 512 + (v + 1) * P],
+                    ident[:],
+                )
+            return bank
+
+        def prep_x(i):
+            src = xt[i][:].bitcast(F32)
+            grp = gpool.tile([P, SLOTS * FEAT], BF16, name="grp", align_bytes=64)
+            grp_v = grp[:].bitcast(F32).rearrange("p (g h q u) -> p g h q u", g=2, h=SLOTS, q=P, u=2)
+            banks = [transposes(src, s) for s in range(SLOTS)]
+            nvec = VEC_COPIES[i]
+            for s in range(SLOTS):
+                copy_out(
+                    s >= SLOTS - nvec,
+                    grp_v[:, :, s, :, :],
+                    banks[s][:].rearrange("p (g u q) -> p g q u", g=2, u=2, q=P),
+                )
+            codes = cpool.tile([P, SLOTS * FEAT // 4], U32, name="codes", align_bytes=64)
+            scales = cpool.tile([P, SLOTS * FEAT // 4], U8, name="scales", align_bytes=64)
+            nc.vector.quantize_mx(out=codes[:].bitcast(FP8X4), scales=scales[:], in_=grp[:])
+            state[i] = (codes, scales)
+
+        def prep_w1():
+            src = w1raw[:].bitcast(F32)
+            grp_v = w1grp[:].bitcast(F32).rearrange("p (j g m u) -> p j g m u", j=SLOTS, g=2, m=P, u=2)
+            for j in range(SLOTS):
+                bank = transposes(src, j)
+                copy_out(False, grp_v[:, j, :, :, :], bank[:].rearrange("p (g u m) -> p g m u", g=2, u=2, m=P))
+                nc.vector.quantize_mx(
+                    out=w1codes[:, j * 256 : (j + 1) * 256].bitcast(FP8X4),
+                    scales=w1scales[:, j * 256 : (j + 1) * 256],
+                    in_=w1grp[:, j * FEAT : (j + 1) * FEAT],
+                )
+
+        def prep_small():
+            src = w2raw[:].bitcast(F32).rearrange("p (w u) -> p u w", u=2)
+            bank = tpool.tile([P, 512], F32, name="bank")
+            for u in range(2):
+                nc.tensor.transpose(bank[:, u * P : (u + 1) * P], src[:, u, :], ident[:])
+            nc.vector.tensor_copy(
+                out=w2grp[:].bitcast(F32).rearrange("p (o u) -> p o u", u=2),
+                in_=bank[:, 0 : 2 * P].rearrange("p (u o) -> p o u", u=2),
+            )
+            nc.vector.tensor_copy(out=b1f[:], in_=b1raw[:])
+            nc.vector.tensor_copy(out=b2f[:], in_=b2raw[:])
+            nc.vector.quantize_mx(out=w2codes[:].bitcast(FP8X4), scales=w2scales[:], in_=w2grp[:])
+
+        def passes(i):
+            g_, c = divmod(i, 4)
+            if c == 0:
+                accs = []
+                for j in range(SLOTS):
+                    acc = apool.tile([P, 512], F32, name="acc%d" % j)
+                    accs.append(acc)
+                state["acc"] = accs
+            accs = state["acc"]
+            codes, scales = state[i]
+            for j in range(SLOTS):
+                for g in range(2):
+                    w = (j * 2 + g) * P
+                    nc.tensor.matmul_mx(
+                        out=accs[j][:],
+                        lhsT=w1codes[:, w : w + P].bitcast(FP8X4),
+                        lhsT_scale=w1scales[:, w : w + P],
+                        rhs=codes[:, g * 512 : (g + 1) * 512].bitcast(FP8X4),
+                        rhs_scale=scales[:, g * 512 : (g + 1) * 512],
+                        start=(c == 0 and g == 0),
+                        stop=(c == 3 and g == 1),
+                    )
+
+        def hidden(grp_i):
+            accs = state["acc"]
+            sums = epool.tile([P, P], F32, name="sums")
+            for j in range(SLOTS):
+                nc.vector.tensor_reduce(
+                    out=sums[:, j * 32 : (j + 1) * 32],
+                    in_=accs[j][:].rearrange("p (h b l) -> p b h l", h=SLOTS, b=32, l=4),
+                    axis=AX.XY,
+                    op=ALU.add,
+                )
+            pre = epool.tile([P, P], F32, name="pre")
+            nc.vector.scalar_tensor_tensor(
+                out=pre[:].rearrange("p (j b) -> p j b", j=SLOTS),
+                in0=sums[:].rearrange("p (j b) -> p j b", j=SLOTS),
+                scalar=1.0 / NODES,
+                in1=b1f[:].unsqueeze(2).to_broadcast([P, SLOTS, 32]),
+                op0=ALU.mult,
+                op1=ALU.add,
+            )
+            m1 = epool.tile([P, HID], BF16, name="m1", align_bytes=64)
+            nc.vector.tensor_scalar_max(
+                out=m1[:].rearrange("p (b r j) -> p b r j", b=32, r=4, j=SLOTS),
+                in0=pre[:].rearrange("p (j b) -> p b j", j=SLOTS).unsqueeze(2).to_broadcast([P, 32, 4, SLOTS]),
+                scalar1=0.0,
+            )
+            m1codes = epool.tile([P, P], U32, name="m1codes", align_bytes=64)
+            m1scales = epool.tile([P, P], U8, name="m1scales", align_bytes=64)
+            nc.vector.quantize_mx(out=m1codes[:].bitcast(FP8X4), scales=m1scales[:], in_=m1[:])
+            state["m1"] = (m1codes, m1scales)
+
+        def second(grp_i):
+            m1codes, m1scales = state["m1"]
+            bank = tpool.tile([P, 512], F32, name="bank")
+            nc.tensor.matmul_mx(
+                out=bank[:, 0:OUTF],
+                lhsT=m1codes[:].bitcast(FP8X4),
+                lhsT_scale=m1scales[:],
+                rhs=w2codes[:].bitcast(FP8X4),
+                rhs_scale=w2scales[:],
+                start=True,
+                stop=True,
+            )
+            pre2 = epool.tile([P, OUTF], F32, name="pre2")
+            nc.vector.tensor_tensor(out=pre2[:], in0=bank[:, 0:OUTF], in1=b2f[:], op=ALU.add)
+            rep_a = epool.tile([P, 8 * OUTF], F32, name="rep_a")
+            rep_b = epool.tile([P, 8 * OUTF], F32, name="rep_b")
+            spread = pre2[:].unsqueeze(1).to_broadcast([P, 8, OUTF])
+            nc.vector.tensor_scalar_max(
+                out=rep_a[:].rearrange("p (n o) -> p n o", n=8), in0=spread, scalar1=0.0
+            )
+            nc.scalar.activation(out=rep_b[:].rearrange("p (n o) -> p n o", n=8), in_=spread, func=ACT.Relu)
+            nc.sync.dma_start(out=ov[grp_i, :, 0 : 8 * OUTF], in_=rep_a[:])
+            nc.sync.dma_start(out=ov[grp_i, :, 8 * OUTF : 16 * OUTF], in_=rep_b[:])
+
+        prep_x(0)
+        prep_w1()
+        passes(0)
+        prep_x(1)
+        for i in range(1, UNITS):
+            if i + 1 < UNITS:
+                prep_x(i + 1)
+            if i == 2:
+                prep_small()
+            passes(i)
+            if i % 4 == 0:
+                second(i // 4 - 1)
+            if i % 4 == 3:
+                hidden(i // 4)
+        second(GROUPS - 1)

@@ -9,7 +9,6 @@ U32 = mybir.dt.uint32
 U8 = mybir.dt.uint8
 FP8X4 = mybir.dt.float8_e4m3fn_x4
 ALU = mybir.AluOpType
-ACT = mybir.ActivationFunctionType
 AX = mybir.AxisListType
 
 P = 128
@@ -23,7 +22,7 @@ SLOTS = 4
 
 FLOPS = 2 * 8192 * FEAT * HID + 2 * 128 * HID * OUTF
 
-VEC_COPIES = [2, 1, 1, 1, 1, 0, 1, 1, 1, 0, 1, 1, 1, 0, 1, 1]
+VEC_COPIES = [2, 2, 2, 2, 1, 1, 0, 1, 1, 1, 0, 1, 1, 1, 0, 1]
 
 
 def tile_gcn_pa_t_kernel(tc, x, W1g, b1g, W2g, b2g, out):
@@ -32,7 +31,7 @@ def tile_gcn_pa_t_kernel(tc, x, W1g, b1g, W2g, b2g, out):
     with ctx:
         const = ctx.enter_context(tc.tile_pool(name="const", bufs=1))
         xpool = ctx.enter_context(tc.tile_pool(name="xpool", bufs=UNITS))
-        gpool = ctx.enter_context(tc.tile_pool(name="gpool", bufs=2))
+        gpool = ctx.enter_context(tc.tile_pool(name="gpool", bufs=3))
         cpool = ctx.enter_context(tc.tile_pool(name="cpool", bufs=3))
         epool = ctx.enter_context(tc.tile_pool(name="epool", bufs=2))
         tpool = ctx.enter_context(tc.psum_pool(name="tpool", bufs=4))
@@ -44,10 +43,6 @@ def tile_gcn_pa_t_kernel(tc, x, W1g, b1g, W2g, b2g, out):
 
         ident = const.tile([P, P], F32)
         make_identity(nc, ident[:])
-        warm = const.tile([P, 1], F32)
-        warm2 = const.tile([P, 1], F32)
-        nc.vector.memset(warm[:], 0.0)
-        nc.scalar.activation(out=warm2[:], in_=warm[:], func=ACT.Relu)
 
         xt = []
         for i in range(UNITS):
@@ -117,6 +112,10 @@ def tile_gcn_pa_t_kernel(tc, x, W1g, b1g, W2g, b2g, out):
                     grp_v[:, :, s, :, :],
                     banks[s][:].rearrange("p (g u q) -> p g q u", g=2, u=2, q=P),
                 )
+            state["grp%d" % i] = grp
+
+        def quant_x(i):
+            grp = state["grp%d" % i]
             codes = cpool.tile([P, SLOTS * FEAT // 4], U32, name="codes", align_bytes=64)
             scales = cpool.tile([P, SLOTS * FEAT // 4], U8, name="scales", align_bytes=64)
             nc.vector.quantize_mx(out=codes[:].bitcast(FP8X4), scales=scales[:], in_=grp[:])
@@ -214,23 +213,25 @@ def tile_gcn_pa_t_kernel(tc, x, W1g, b1g, W2g, b2g, out):
             )
             pre2 = epool.tile([P, OUTF], F32, name="pre2")
             nc.vector.tensor_tensor(out=pre2[:], in0=bank[:, 0:OUTF], in1=b2f[:], op=ALU.add)
-            rep_a = epool.tile([P, 8 * OUTF], F32, name="rep_a")
-            rep_b = epool.tile([P, 8 * OUTF], F32, name="rep_b")
-            spread = pre2[:].unsqueeze(1).to_broadcast([P, 8, OUTF])
-            nc.vector.tensor_scalar_max(
-                out=rep_a[:].rearrange("p (n o) -> p n o", n=8), in0=spread, scalar1=0.0
+            m2 = epool.tile([P, OUTF], F32, name="m2")
+            nc.vector.tensor_scalar_max(out=m2[:], in0=pre2[:], scalar1=0.0)
+            nc.sync.dma_start(
+                out=ov[grp_i].rearrange("q (n o) -> q n o", n=16),
+                in_=m2[:].unsqueeze(1).to_broadcast([P, 16, OUTF]),
             )
-            nc.scalar.activation(out=rep_b[:].rearrange("p (n o) -> p n o", n=8), in_=spread, func=ACT.Relu)
-            nc.sync.dma_start(out=ov[grp_i, :, 0 : 8 * OUTF], in_=rep_a[:])
-            nc.sync.dma_start(out=ov[grp_i, :, 8 * OUTF : 16 * OUTF], in_=rep_b[:])
 
         prep_x(0)
+        quant_x(0)
         prep_w1()
         passes(0)
         prep_x(1)
+        quant_x(1)
+        prep_x(2)
         for i in range(1, UNITS):
             if i + 1 < UNITS:
-                prep_x(i + 1)
+                quant_x(i + 1)
+            if i + 2 < UNITS:
+                prep_x(i + 2)
             if i == 2:
                 prep_small()
             passes(i)

@@ -16,13 +16,36 @@ NODES = 64
 FEAT = 1024
 HID = 512
 OUTF = 128
-GROUPS = 4
-UNITS = 16
 SLOTS = 4
+UNITS = 16
+UNIT_COLS = SLOTS * FEAT
+UNIT_WORDS = UNIT_COLS // 4
+PASSES = 8
 
 FLOPS = 2 * 8192 * FEAT * HID + 2 * 128 * HID * OUTF
 
-VEC_COPIES = [2, 2, 2, 2, 1, 1, 0, 1, 1, 1, 0, 1, 1, 1, 0, 1]
+GROUP_UNITS = (8, 4, 2, 2)
+HEAD_STEPS = ((4, 4), (4, 4), (4, 4), (4, 4))
+RUN_SLOTS = 4
+SECOND_LAG = 16
+SMALL_LOADS_AFTER = 6
+SMALL_STEP = 7
+VECTOR_HEAD_SLOTS = 16
+
+
+def plan_steps():
+    steps = list(HEAD_STEPS)
+    slots = sum([a for a, b in steps])
+    passes = sum([b for a, b in steps])
+    while slots < UNITS * SLOTS:
+        a = min(RUN_SLOTS, UNITS * SLOTS - slots)
+        steps.append((a, 2 * a))
+        slots += a
+        passes += 2 * a
+    while passes < UNITS * PASSES:
+        steps.append((0, PASSES))
+        passes += PASSES
+    return steps
 
 
 def tile_gcn_pa_t_kernel(tc, x, W1g, b1g, W2g, b2g, out):
@@ -32,63 +55,73 @@ def tile_gcn_pa_t_kernel(tc, x, W1g, b1g, W2g, b2g, out):
         const = ctx.enter_context(tc.tile_pool(name="const", bufs=1))
         xpool = ctx.enter_context(tc.tile_pool(name="xpool", bufs=UNITS))
         gpool = ctx.enter_context(tc.tile_pool(name="gpool", bufs=3))
-        cpool = ctx.enter_context(tc.tile_pool(name="cpool", bufs=3))
+        cpool = ctx.enter_context(tc.tile_pool(name="cpool", bufs=4))
         epool = ctx.enter_context(tc.tile_pool(name="epool", bufs=2))
         tpool = ctx.enter_context(tc.psum_pool(name="tpool", bufs=4))
         apool = ctx.enter_context(tc.psum_pool(name="apool", bufs=1))
         ctx.enter_context(tc.manual_schedule())
 
-        xv = x.flatten_outer_dims().rearrange("(g q s) f -> g q (s f)", g=GROUPS, q=P)
-        ov = out.flatten_outer_dims().rearrange("(g q s) o -> g q (s o)", g=GROUPS, q=P)
+        unit_group = []
+        unit_pos = []
+        x_views = []
+        o_views = []
+        x_rows = x.flatten_outer_dims()
+        o_rows = out.flatten_outer_dims()
+        row0 = 0
+        for grp_i, n_units in enumerate(GROUP_UNITS):
+            rows = n_units * SLOTS * P
+            x_views.append(x_rows[row0 : row0 + rows, :].rearrange("(q s) f -> q (s f)", q=P))
+            o_views.append(o_rows[row0 : row0 + rows, :].rearrange("(q s) o -> q s o", q=P))
+            row0 += rows
+            for c in range(n_units):
+                unit_group.append(grp_i)
+                unit_pos.append(c)
 
         ident = const.tile([P, P], F32)
         make_identity(nc, ident[:])
 
         xt = []
         for i in range(UNITS):
-            x_sb = xpool.tile([P, SLOTS * FEAT], BF16, name="x_sb")
+            x_sb = xpool.tile([P, UNIT_COLS], BF16, name="x_sb")
             xt.append(x_sb)
-        w1raw = const.tile([P, SLOTS * FEAT], BF16)
+        w1raw = const.tile([P, UNIT_COLS], BF16)
         w1v = W1g.rearrange("(p j) k -> p (j k)", j=SLOTS)
+        w2raw = const.tile([P, HID], BF16)
+        b1raw = const.tile([P, SLOTS], BF16)
+        b2raw = const.tile([P, OUTF], BF16)
 
         def load_x(i, pieces):
-            g, c = divmod(i, 4)
-            w = SLOTS * FEAT // pieces
+            c0 = unit_pos[i] * UNIT_COLS
+            w = UNIT_COLS // pieces
             for s in range(pieces):
                 nc.sync.dma_start(
                     out=xt[i][:, s * w : (s + 1) * w],
-                    in_=xv[g, :, c * SLOTS * FEAT + s * w : c * SLOTS * FEAT + (s + 1) * w],
+                    in_=x_views[unit_group[i]][:, c0 + s * w : c0 + (s + 1) * w],
                 )
 
-        load_x(0, 4)
+        load_x(0, SLOTS)
         for j in range(SLOTS):
             nc.sync.dma_start(out=w1raw[:, j * FEAT : (j + 1) * FEAT], in_=w1v[:, j * FEAT : (j + 1) * FEAT])
         for i in range(1, UNITS):
             load_x(i, 1)
+            if i == SMALL_LOADS_AFTER:
+                nc.sync.dma_start(out=w2raw[:], in_=W2g)
+                nc.sync.dma_start(out=b1raw[:], in_=b1g.rearrange("(p j) -> p j", j=SLOTS))
+                nc.sync.dma_start(out=b2raw[:], in_=b2g.partition_broadcast(P))
 
-        w2raw = const.tile([P, HID], BF16)
-        nc.scalar.dma_start(out=w2raw[:], in_=W2g)
-        b1raw = const.tile([P, SLOTS], BF16)
-        nc.scalar.dma_start(out=b1raw[:], in_=b1g.rearrange("(p j) -> p j", j=SLOTS))
-        b2raw = const.tile([P, OUTF], BF16)
-        nc.scalar.dma_start(out=b2raw[:], in_=b2g.partition_broadcast(P))
-
-        w1grp = const.tile([P, SLOTS * FEAT], BF16, align_bytes=64)
-        w1codes = const.tile([P, SLOTS * FEAT // 4], U32, align_bytes=64)
-        w1scales = const.tile([P, SLOTS * FEAT // 4], U8, align_bytes=64)
+        w1grp = const.tile([P, UNIT_COLS], BF16, align_bytes=64)
+        w1codes = const.tile([P, UNIT_WORDS], U32, align_bytes=64)
+        w1scales = const.tile([P, UNIT_WORDS], U8, align_bytes=64)
         w2grp = const.tile([P, HID], BF16, align_bytes=64)
         w2codes = const.tile([P, OUTF], U32, align_bytes=64)
         w2scales = const.tile([P, OUTF], U8, align_bytes=64)
         b1f = const.tile([P, SLOTS], F32)
         b2f = const.tile([P, OUTF], F32)
 
-        state = {}
-
-        def copy_out(engine_is_vector, dst, src):
-            if engine_is_vector:
-                nc.vector.tensor_copy(out=dst, in_=src)
-            else:
-                nc.scalar.copy(out=dst, in_=src)
+        grouped = {}
+        quantised = {}
+        accs = {}
+        hidden_codes = {}
 
         def transposes(src_f32, s):
             bank = tpool.tile([P, 512], F32, name="bank")
@@ -100,33 +133,30 @@ def tile_gcn_pa_t_kernel(tc, x, W1g, b1g, W2g, b2g, out):
                 )
             return bank
 
-        def prep_x(i):
-            src = xt[i][:].bitcast(F32)
-            grp = gpool.tile([P, SLOTS * FEAT], BF16, name="grp", align_bytes=64)
-            grp_v = grp[:].bitcast(F32).rearrange("p (g h q u) -> p g h q u", g=2, h=SLOTS, q=P, u=2)
-            banks = [transposes(src, s) for s in range(SLOTS)]
-            nvec = VEC_COPIES[i]
-            for s in range(SLOTS):
-                copy_out(
-                    s >= SLOTS - nvec,
-                    grp_v[:, :, s, :, :],
-                    banks[s][:].rearrange("p (g u q) -> p g q u", g=2, u=2, q=P),
-                )
-            state["grp%d" % i] = grp
+        def copy_slot(slot, bank):
+            i, s = divmod(slot, SLOTS)
+            if s == 0:
+                grp = gpool.tile([P, UNIT_COLS], BF16, name="grp", align_bytes=64)
+                grouped[i] = grp
+            dst = grouped[i][:].bitcast(F32).rearrange("p (g h q u) -> p g h q u", g=2, h=SLOTS, q=P, u=2)
+            src = bank[:].rearrange("p (g u q) -> p g q u", g=2, u=2, q=P)
+            if slot < VECTOR_HEAD_SLOTS and slot % 2 == 1:
+                nc.vector.tensor_copy(out=dst[:, :, s, :, :], in_=src)
+            else:
+                nc.scalar.copy(out=dst[:, :, s, :, :], in_=src)
 
         def quant_x(i):
-            grp = state["grp%d" % i]
-            codes = cpool.tile([P, SLOTS * FEAT // 4], U32, name="codes", align_bytes=64)
-            scales = cpool.tile([P, SLOTS * FEAT // 4], U8, name="scales", align_bytes=64)
-            nc.vector.quantize_mx(out=codes[:].bitcast(FP8X4), scales=scales[:], in_=grp[:])
-            state[i] = (codes, scales)
+            codes = cpool.tile([P, UNIT_WORDS], U32, name="codes", align_bytes=64)
+            scales = cpool.tile([P, UNIT_WORDS], U8, name="scales", align_bytes=64)
+            nc.vector.quantize_mx(out=codes[:].bitcast(FP8X4), scales=scales[:], in_=grouped[i][:])
+            quantised[i] = (codes, scales)
 
         def prep_w1():
             src = w1raw[:].bitcast(F32)
             grp_v = w1grp[:].bitcast(F32).rearrange("p (j g m u) -> p j g m u", j=SLOTS, g=2, m=P, u=2)
             for j in range(SLOTS):
                 bank = transposes(src, j)
-                copy_out(False, grp_v[:, j, :, :, :], bank[:].rearrange("p (g u m) -> p g m u", g=2, u=2, m=P))
+                nc.scalar.copy(out=grp_v[:, j, :, :, :], in_=bank[:].rearrange("p (g u m) -> p g m u", g=2, u=2, m=P))
                 nc.vector.quantize_mx(
                     out=w1codes[:, j * 256 : (j + 1) * 256].bitcast(FP8X4),
                     scales=w1scales[:, j * 256 : (j + 1) * 256],
@@ -146,61 +176,66 @@ def tile_gcn_pa_t_kernel(tc, x, W1g, b1g, W2g, b2g, out):
             nc.vector.tensor_copy(out=b2f[:], in_=b2raw[:])
             nc.vector.quantize_mx(out=w2codes[:].bitcast(FP8X4), scales=w2scales[:], in_=w2grp[:])
 
-        def passes(i):
-            g_, c = divmod(i, 4)
-            if c == 0:
-                accs = []
-                for j in range(SLOTS):
-                    acc = apool.tile([P, 512], F32, name="acc%d" % j)
-                    accs.append(acc)
-                state["acc"] = accs
-            accs = state["acc"]
-            codes, scales = state[i]
-            for j in range(SLOTS):
-                for g in range(2):
-                    w = (j * 2 + g) * P
-                    nc.tensor.matmul_mx(
-                        out=accs[j][:],
-                        lhsT=w1codes[:, w : w + P].bitcast(FP8X4),
-                        lhsT_scale=w1scales[:, w : w + P],
-                        rhs=codes[:, g * 512 : (g + 1) * 512].bitcast(FP8X4),
-                        rhs_scale=scales[:, g * 512 : (g + 1) * 512],
-                        start=(c == 0 and g == 0),
-                        stop=(c == 3 and g == 1),
-                    )
+        def one_pass(n):
+            i, r = divmod(n, PASSES)
+            j, g = divmod(r, 2)
+            first = unit_pos[i] == 0
+            last = unit_pos[i] == GROUP_UNITS[unit_group[i]] - 1
+            if first and g == 0:
+                acc = apool.tile([P, 512], F32, name="acc%d" % j)
+                accs[j] = acc
+            codes, scales = quantised[i]
+            w = (j * 2 + g) * P
+            nc.tensor.matmul_mx(
+                out=accs[j][:],
+                lhsT=w1codes[:, w : w + P].bitcast(FP8X4),
+                lhsT_scale=w1scales[:, w : w + P],
+                rhs=codes[:, g * 512 : (g + 1) * 512].bitcast(FP8X4),
+                rhs_scale=scales[:, g * 512 : (g + 1) * 512],
+                start=(first and g == 0),
+                stop=(last and g == 1),
+            )
 
-        def hidden(grp_i):
-            accs = state["acc"]
-            sums = epool.tile([P, P], F32, name="sums")
+        def node_sums(grp_i):
+            nb = 8 * GROUP_UNITS[grp_i]
+            sums = epool.tile([P, 256], F32, name="sums")
             for j in range(SLOTS):
                 nc.vector.tensor_reduce(
-                    out=sums[:, j * 32 : (j + 1) * 32],
-                    in_=accs[j][:].rearrange("p (h b l) -> p b h l", h=SLOTS, b=32, l=4),
+                    out=sums[:, j * nb : (j + 1) * nb],
+                    in_=accs[j][:].rearrange("p (h b l) -> p b h l", h=SLOTS, b=nb, l=P // nb),
                     axis=AX.XY,
                     op=ALU.add,
                 )
-            pre = epool.tile([P, P], F32, name="pre")
+            hidden_codes[grp_i] = sums
+
+        def hidden(grp_i):
+            nb = 8 * GROUP_UNITS[grp_i]
+            sums = hidden_codes[grp_i]
+            pre = epool.tile([P, 256], F32, name="pre")
             nc.vector.scalar_tensor_tensor(
-                out=pre[:].rearrange("p (j b) -> p j b", j=SLOTS),
-                in0=sums[:].rearrange("p (j b) -> p j b", j=SLOTS),
+                out=pre[:, 0 : SLOTS * nb].rearrange("p (j b) -> p j b", j=SLOTS),
+                in0=sums[:, 0 : SLOTS * nb].rearrange("p (j b) -> p j b", j=SLOTS),
                 scalar=1.0 / NODES,
-                in1=b1f[:].unsqueeze(2).to_broadcast([P, SLOTS, 32]),
+                in1=b1f[:].unsqueeze(2).to_broadcast([P, SLOTS, nb]),
                 op0=ALU.mult,
                 op1=ALU.add,
             )
             m1 = epool.tile([P, HID], BF16, name="m1", align_bytes=64)
             nc.vector.tensor_scalar_max(
-                out=m1[:].rearrange("p (b r j) -> p b r j", b=32, r=4, j=SLOTS),
-                in0=pre[:].rearrange("p (j b) -> p b j", j=SLOTS).unsqueeze(2).to_broadcast([P, 32, 4, SLOTS]),
+                out=m1[:].rearrange("p (b r j) -> p b r j", b=nb, r=P // nb, j=SLOTS),
+                in0=pre[:, 0 : SLOTS * nb]
+                .rearrange("p (j b) -> p b j", j=SLOTS)
+                .unsqueeze(2)
+                .to_broadcast([P, nb, P // nb, SLOTS]),
                 scalar1=0.0,
             )
             m1codes = epool.tile([P, P], U32, name="m1codes", align_bytes=64)
             m1scales = epool.tile([P, P], U8, name="m1scales", align_bytes=64)
             nc.vector.quantize_mx(out=m1codes[:].bitcast(FP8X4), scales=m1scales[:], in_=m1[:])
-            state["m1"] = (m1codes, m1scales)
+            hidden_codes[grp_i] = (m1codes, m1scales)
 
         def second(grp_i):
-            m1codes, m1scales = state["m1"]
+            m1codes, m1scales = hidden_codes[grp_i]
             bank = tpool.tile([P, 512], F32, name="bank")
             nc.tensor.matmul_mx(
                 out=bank[:, 0:OUTF],
@@ -215,28 +250,46 @@ def tile_gcn_pa_t_kernel(tc, x, W1g, b1g, W2g, b2g, out):
             nc.vector.tensor_tensor(out=pre2[:], in0=bank[:, 0:OUTF], in1=b2f[:], op=ALU.add)
             m2 = epool.tile([P, OUTF], F32, name="m2")
             nc.vector.tensor_scalar_max(out=m2[:], in0=pre2[:], scalar1=0.0)
-            nc.sync.dma_start(
-                out=ov[grp_i].rearrange("q (n o) -> q n o", n=16),
-                in_=m2[:].unsqueeze(1).to_broadcast([P, 16, OUTF]),
-            )
+            n_rep = SLOTS * GROUP_UNITS[grp_i]
+            nc.sync.dma_start(out=o_views[grp_i], in_=m2[:].unsqueeze(1).to_broadcast([P, n_rep, OUTF]))
 
-        prep_x(0)
-        quant_x(0)
-        prep_w1()
-        passes(0)
-        prep_x(1)
-        quant_x(1)
-        prep_x(2)
-        for i in range(1, UNITS):
-            if i + 1 < UNITS:
-                quant_x(i + 1)
-            if i + 2 < UNITS:
-                prep_x(i + 2)
-            if i == 2:
+        n_slots = 0
+        n_passes = 0
+        n_quant = 0
+        to_hide = []
+        to_second = []
+        for step, (run_slots, run_passes) in enumerate(plan_steps()):
+            while n_quant < UNITS and SLOTS * (n_quant + 1) <= n_slots:
+                quant_x(n_quant)
+                n_quant += 1
+            for grp_i in to_hide:
+                hidden(grp_i)
+            to_hide = []
+            banks = []
+            for k in range(run_slots):
+                i, s = divmod(n_slots + k, SLOTS)
+                banks.append(transposes(xt[i][:].bitcast(F32), s))
+            for k in range(run_slots):
+                copy_slot(n_slots + k, banks[k])
+            n_slots += run_slots
+            if step == 0:
+                quant_x(0)
+                n_quant = 1
+                prep_w1()
+            if step == SMALL_STEP:
                 prep_small()
-            passes(i)
-            if i % 4 == 0:
-                second(i // 4 - 1)
-            if i % 4 == 3:
-                hidden(i // 4)
-        second(GROUPS - 1)
+            for k in range(run_passes):
+                one_pass(n_passes)
+                n_passes += 1
+                i = n_passes // PASSES - 1
+                if n_passes % PASSES == 0 and unit_pos[i] == GROUP_UNITS[unit_group[i]] - 1:
+                    node_sums(unit_group[i])
+                    to_hide.append(unit_group[i])
+                    to_second.append((unit_group[i], n_passes))
+            if n_passes == UNITS * PASSES:
+                for grp_i in to_hide:
+                    hidden(grp_i)
+                to_hide = []
+            while to_second and (n_passes - to_second[0][1] >= SECOND_LAG or n_passes == UNITS * PASSES):
+                second(to_second[0][0])
+                to_second = to_second[1:]

@@ -25,9 +25,11 @@ PASSES = 8
 FLOPS = 2 * 8192 * FEAT * HID + 2 * 128 * HID * OUTF
 
 GROUP_UNITS = (8, 4, 2, 2)
-HEAD_STEPS = ((4, 4), (4, 4), (4, 4), (4, 4))
+NARROW_GROUPS = (2, 3)
+HEAD_STEPS = ((4, 4),) * 6
 RUN_SLOTS = 4
-SECOND_LAG = 16
+SECOND_LAG = (16, 16, 12, 0)
+TAIL_STEP = 4
 SMALL_LOADS_AFTER = 6
 SMALL_STEP = 7
 VECTOR_HEAD_SLOTS = 16
@@ -43,9 +45,22 @@ def plan_steps():
         slots += a
         passes += 2 * a
     while passes < UNITS * PASSES:
-        steps.append((0, PASSES))
-        passes += PASSES
+        steps.append((0, TAIL_STEP))
+        passes += TAIL_STEP
     return steps
+
+
+def plan_passes():
+    order = []
+    unit0 = 0
+    for grp_i, n_units in enumerate(GROUP_UNITS):
+        units = range(unit0, unit0 + n_units)
+        if grp_i == len(GROUP_UNITS) - 1:
+            order.extend([(grp_i, i, j, g) for j in range(SLOTS) for i in units for g in range(2)])
+        else:
+            order.extend([(grp_i, i, j, g) for i in units for j in range(SLOTS) for g in range(2)])
+        unit0 += n_units
+    return order
 
 
 def tile_gcn_pa_t_kernel(tc, x, W1g, b1g, W2g, b2g, out):
@@ -55,7 +70,7 @@ def tile_gcn_pa_t_kernel(tc, x, W1g, b1g, W2g, b2g, out):
         const = ctx.enter_context(tc.tile_pool(name="const", bufs=1))
         xpool = ctx.enter_context(tc.tile_pool(name="xpool", bufs=UNITS))
         gpool = ctx.enter_context(tc.tile_pool(name="gpool", bufs=3))
-        cpool = ctx.enter_context(tc.tile_pool(name="cpool", bufs=4))
+        cpool = ctx.enter_context(tc.tile_pool(name="cpool", bufs=5))
         epool = ctx.enter_context(tc.tile_pool(name="epool", bufs=2))
         tpool = ctx.enter_context(tc.psum_pool(name="tpool", bufs=4))
         apool = ctx.enter_context(tc.psum_pool(name="apool", bufs=1))
@@ -121,6 +136,7 @@ def tile_gcn_pa_t_kernel(tc, x, W1g, b1g, W2g, b2g, out):
         grouped = {}
         quantised = {}
         accs = {}
+        hidden_parts = {}
         hidden_codes = {}
 
         def transposes(src_f32, s):
@@ -176,59 +192,56 @@ def tile_gcn_pa_t_kernel(tc, x, W1g, b1g, W2g, b2g, out):
             nc.vector.tensor_copy(out=b2f[:], in_=b2raw[:])
             nc.vector.quantize_mx(out=w2codes[:].bitcast(FP8X4), scales=w2scales[:], in_=w2grp[:])
 
-        def one_pass(n):
-            i, r = divmod(n, PASSES)
-            j, g = divmod(r, 2)
-            first = unit_pos[i] == 0
-            last = unit_pos[i] == GROUP_UNITS[unit_group[i]] - 1
-            if first and g == 0:
+        def one_pass(grp_i, i, j, g):
+            first = unit_pos[i] == 0 and g == 0
+            last = unit_pos[i] == GROUP_UNITS[grp_i] - 1 and g == 1
+            if first:
                 acc = apool.tile([P, 512], F32, name="acc%d" % j)
                 accs[j] = acc
             codes, scales = quantised[i]
             w = (j * 2 + g) * P
-            nc.tensor.matmul_mx(
-                out=accs[j][:],
-                lhsT=w1codes[:, w : w + P].bitcast(FP8X4),
-                lhsT_scale=w1scales[:, w : w + P],
-                rhs=codes[:, g * 512 : (g + 1) * 512].bitcast(FP8X4),
-                rhs_scale=scales[:, g * 512 : (g + 1) * 512],
-                start=(first and g == 0),
-                stop=(last and g == 1),
-            )
-
-        def node_sums(grp_i):
-            nb = 8 * GROUP_UNITS[grp_i]
-            sums = epool.tile([P, 256], F32, name="sums")
-            for j in range(SLOTS):
-                nc.vector.tensor_reduce(
-                    out=sums[:, j * nb : (j + 1) * nb],
-                    in_=accs[j][:].rearrange("p (h b l) -> p b h l", h=SLOTS, b=nb, l=P // nb),
-                    axis=AX.XY,
-                    op=ALU.add,
+            parts = 2 if grp_i in NARROW_GROUPS else 1
+            width = 512 // parts
+            for part in range(parts):
+                c0 = g * 512 + part * width
+                nc.tensor.matmul_mx(
+                    out=accs[j][:, 0:width],
+                    lhsT=w1codes[:, w : w + P].bitcast(FP8X4),
+                    lhsT_scale=w1scales[:, w : w + P],
+                    rhs=codes[:, c0 : c0 + width].bitcast(FP8X4),
+                    rhs_scale=scales[:, c0 : c0 + width],
+                    start=(first and part == 0),
+                    stop=(last and part == parts - 1),
                 )
-            hidden_codes[grp_i] = sums
+            return last
 
-        def hidden(grp_i):
+        def node_sum(grp_i, j):
             nb = 8 * GROUP_UNITS[grp_i]
-            sums = hidden_codes[grp_i]
-            pre = epool.tile([P, 256], F32, name="pre")
-            nc.vector.scalar_tensor_tensor(
-                out=pre[:, 0 : SLOTS * nb].rearrange("p (j b) -> p j b", j=SLOTS),
-                in0=sums[:, 0 : SLOTS * nb].rearrange("p (j b) -> p j b", j=SLOTS),
-                scalar=1.0 / NODES,
-                in1=b1f[:].unsqueeze(2).to_broadcast([P, SLOTS, nb]),
+            parts = 2 if grp_i in NARROW_GROUPS else 1
+            if j == 0:
+                sums = epool.tile([P, 256], F32, name="sums")
+                m1pre = epool.tile([P, HID], BF16, name="m1pre")
+                hidden_parts[grp_i] = (sums, m1pre)
+            sums, m1pre = hidden_parts[grp_i]
+            nc.vector.tensor_reduce(
+                out=sums[:, j * nb : (j + 1) * nb],
+                in_=accs[j][:, 0 : 512 // parts].rearrange("p (h b l) -> p b h l", h=SLOTS // parts, b=nb, l=P // nb),
+                axis=AX.XY,
+                op=ALU.add,
+            )
+            nc.vector.tensor_scalar(
+                out=m1pre[:].rearrange("p (b r j) -> p b r j", b=nb, r=P // nb, j=SLOTS)[:, :, :, j],
+                in0=sums[:, j * nb : (j + 1) * nb].unsqueeze(2).to_broadcast([P, nb, P // nb]),
+                scalar1=1.0 / NODES,
+                scalar2=b1f[:, j : j + 1],
                 op0=ALU.mult,
                 op1=ALU.add,
             )
+
+        def hidden(grp_i):
+            m1pre = hidden_parts[grp_i][1]
             m1 = epool.tile([P, HID], BF16, name="m1", align_bytes=64)
-            nc.vector.tensor_scalar_max(
-                out=m1[:].rearrange("p (b r j) -> p b r j", b=nb, r=P // nb, j=SLOTS),
-                in0=pre[:, 0 : SLOTS * nb]
-                .rearrange("p (j b) -> p b j", j=SLOTS)
-                .unsqueeze(2)
-                .to_broadcast([P, nb, P // nb, SLOTS]),
-                scalar1=0.0,
-            )
+            nc.vector.tensor_scalar_max(out=m1[:], in0=m1pre[:], scalar1=0.0)
             m1codes = epool.tile([P, P], U32, name="m1codes", align_bytes=64)
             m1scales = epool.tile([P, P], U8, name="m1scales", align_bytes=64)
             nc.vector.quantize_mx(out=m1codes[:].bitcast(FP8X4), scales=m1scales[:], in_=m1[:])
@@ -253,6 +266,7 @@ def tile_gcn_pa_t_kernel(tc, x, W1g, b1g, W2g, b2g, out):
             n_rep = SLOTS * GROUP_UNITS[grp_i]
             nc.sync.dma_start(out=o_views[grp_i], in_=m2[:].unsqueeze(1).to_broadcast([P, n_rep, OUTF]))
 
+        pass_order = plan_passes()
         n_slots = 0
         n_passes = 0
         n_quant = 0
@@ -279,17 +293,20 @@ def tile_gcn_pa_t_kernel(tc, x, W1g, b1g, W2g, b2g, out):
             if step == SMALL_STEP:
                 prep_small()
             for k in range(run_passes):
-                one_pass(n_passes)
+                grp_i, i, j, g = pass_order[n_passes]
+                closes = one_pass(grp_i, i, j, g)
                 n_passes += 1
-                i = n_passes // PASSES - 1
-                if n_passes % PASSES == 0 and unit_pos[i] == GROUP_UNITS[unit_group[i]] - 1:
-                    node_sums(unit_group[i])
-                    to_hide.append(unit_group[i])
-                    to_second.append((unit_group[i], n_passes))
+                if closes:
+                    node_sum(grp_i, j)
+                    if j == SLOTS - 1:
+                        to_hide.append(grp_i)
+                        to_second.append((grp_i, n_passes))
             if n_passes == UNITS * PASSES:
                 for grp_i in to_hide:
                     hidden(grp_i)
                 to_hide = []
-            while to_second and (n_passes - to_second[0][1] >= SECOND_LAG or n_passes == UNITS * PASSES):
+            while to_second and (
+                n_passes - to_second[0][1] >= SECOND_LAG[to_second[0][0]] or n_passes == UNITS * PASSES
+            ):
                 second(to_second[0][0])
                 to_second = to_second[1:]

@@ -27,7 +27,7 @@ FLOPS = 2 * 8192 * FEAT * HID + 2 * 128 * HID * OUTF
 GROUP_UNITS = (8, 4, 2, 2)
 NARROW_GROUPS = (2, 3)
 HEAD_STEPS = ((4, 4),) * 6
-RUN_SLOTS = 4
+RUN_SLOTS = 3
 SECOND_LAG = (16, 16, 12, 0)
 TAIL_STEP = 4
 SMALL_LOADS_AFTER = 6

@@ -27,7 +27,7 @@ FLOPS = 2 * 8192 * FEAT * HID + 2 * 128 * HID * OUTF
 GROUP_UNITS = (8, 4, 2, 2)
 NARROW_GROUPS = (2, 3)
 HEAD_STEPS = ((4, 4),) * 6
-RUN_SLOTS = 3
+RUN_SLOTS = 2
 SECOND_LAG = (16, 16, 12, 0)
 TAIL_STEP = 4
 SMALL_LOADS_AFTER = 6

@@ -26,24 +26,24 @@ FLOPS = 2 * 8192 * FEAT * HID + 2 * 128 * HID * OUTF
 
 GROUP_UNITS = (8, 4, 2, 2)
 NARROW_GROUPS = (2, 3)
-HEAD_STEPS = ((4, 4),) * 6
-RUN_SLOTS = 2
+HEAD_STEPS = ((16, 4), (8, 1), (8, 1), (8, 1), (8, 1), (8, 2), (8, 2), (8, 2), (8, 2))
+RUN_TRANSPOSES = 8
 SECOND_LAG = (16, 16, 12, 0)
 TAIL_STEP = 4
 SMALL_LOADS_AFTER = 6
-SMALL_STEP = 7
+SMALL_STEP = 14
 VECTOR_HEAD_SLOTS = 16
 
 
 def plan_steps():
     steps = list(HEAD_STEPS)
-    slots = sum([a for a, b in steps])
+    transposes = sum([a for a, b in steps])
     passes = sum([b for a, b in steps])
-    while slots < UNITS * SLOTS:
-        a = min(RUN_SLOTS, UNITS * SLOTS - slots)
-        steps.append((a, 2 * a))
-        slots += a
-        passes += 2 * a
+    while transposes < UNITS * SLOTS * 4:
+        a = min(RUN_TRANSPOSES, UNITS * SLOTS * 4 - transposes)
+        steps.append((a, a // 2))
+        transposes += a
+        passes += a // 2
     while passes < UNITS * PASSES:
         steps.append((0, TAIL_STEP))
         passes += TAIL_STEP
@@ -267,25 +267,37 @@ def tile_gcn_pa_t_kernel(tc, x, W1g, b1g, W2g, b2g, out):
             nc.sync.dma_start(out=o_views[grp_i], in_=m2[:].unsqueeze(1).to_broadcast([P, n_rep, OUTF]))
 
         pass_order = plan_passes()
-        n_slots = 0
+        n_transposes = 0
+        n_copied = 0
         n_passes = 0
         n_quant = 0
         to_hide = []
         to_second = []
-        for step, (run_slots, run_passes) in enumerate(plan_steps()):
-            while n_quant < UNITS and SLOTS * (n_quant + 1) <= n_slots:
+        open_bank = None
+        for step, (run_transposes, run_passes) in enumerate(plan_steps()):
+            while n_quant < UNITS and SLOTS * (n_quant + 1) <= n_copied:
                 quant_x(n_quant)
                 n_quant += 1
             for grp_i in to_hide:
                 hidden(grp_i)
             to_hide = []
-            banks = []
-            for k in range(run_slots):
-                i, s = divmod(n_slots + k, SLOTS)
-                banks.append(transposes(xt[i][:].bitcast(F32), s))
-            for k in range(run_slots):
-                copy_slot(n_slots + k, banks[k])
-            n_slots += run_slots
+            filled = []
+            for k in range(run_transposes):
+                slot, v = divmod(n_transposes, 4)
+                i, s = divmod(slot, SLOTS)
+                if v == 0:
+                    open_bank = tpool.tile([P, 512], F32, name="bank")
+                nc.tensor.transpose(
+                    open_bank[:, v * P : (v + 1) * P],
+                    xt[i][:].bitcast(F32)[:, s * 512 + v * P : s * 512 + (v + 1) * P],
+                    ident[:],
+                )
+                if v == 3:
+                    filled.append((slot, open_bank))
+                n_transposes += 1
+            for slot, bank in filled:
+                copy_slot(slot, bank)
+            n_copied += len(filled)
             if step == 0:
                 quant_x(0)
                 n_quant = 1

@@ -26,13 +26,12 @@ FLOPS = 2 * 8192 * FEAT * HID + 2 * 128 * HID * OUTF
 
 GROUP_UNITS = (8, 4, 2, 2)
 NARROW_GROUPS = (2, 3)
-HEAD_STEPS = ((16, 4), (8, 1), (8, 1), (8, 1), (8, 1), (8, 2), (8, 2), (8, 2), (8, 2))
-RUN_TRANSPOSES = 8
+HEAD_STEPS = ((16, 4),) * 6
+RUN_TRANSPOSES = 16
 SECOND_LAG = (16, 16, 12, 0)
 TAIL_STEP = 4
 SMALL_LOADS_AFTER = 6
-SMALL_STEP = 14
-VECTOR_HEAD_SLOTS = 16
+SMALL_STEP = 10
 
 
 def plan_steps():
@@ -41,12 +40,16 @@ def plan_steps():
     passes = sum([b for a, b in steps])
     while transposes < UNITS * SLOTS * 4:
         a = min(RUN_TRANSPOSES, UNITS * SLOTS * 4 - transposes)
-        steps.append((a, a // 2))
+        b = a // 2
+        if len(steps) == SMALL_STEP:
+            a -= 4
+        steps.append((a, b))
         transposes += a
-        passes += a // 2
+        passes += b
     while passes < UNITS * PASSES:
-        steps.append((0, TAIL_STEP))
-        passes += TAIL_STEP
+        b = min(TAIL_STEP, UNITS * PASSES - passes)
+        steps.append((0, b))
+        passes += b
     return steps
 
 
@@ -149,14 +152,14 @@ def tile_gcn_pa_t_kernel(tc, x, W1g, b1g, W2g, b2g, out):
                 )
             return bank
 
-        def copy_slot(slot, bank):
+        def copy_slot(slot, bank, on_vector):
             i, s = divmod(slot, SLOTS)
-            if s == 0:
+            if i not in grouped:
                 grp = gpool.tile([P, UNIT_COLS], BF16, name="grp", align_bytes=64)
                 grouped[i] = grp
             dst = grouped[i][:].bitcast(F32).rearrange("p (g h q u) -> p g h q u", g=2, h=SLOTS, q=P, u=2)
             src = bank[:].rearrange("p (g u q) -> p g q u", g=2, u=2, q=P)
-            if slot < VECTOR_HEAD_SLOTS and slot % 2 == 1:
+            if on_vector:
                 nc.vector.tensor_copy(out=dst[:, :, s, :, :], in_=src)
             else:
                 nc.scalar.copy(out=dst[:, :, s, :, :], in_=src)
@@ -295,8 +298,17 @@ def tile_gcn_pa_t_kernel(tc, x, W1g, b1g, W2g, b2g, out):
                 if v == 3:
                     filled.append((slot, open_bank))
                 n_transposes += 1
-            for slot, bank in filled:
-                copy_slot(slot, bank)
+            closing = False
+            for n in range(n_passes, min(n_passes + run_passes, UNITS * PASSES)):
+                grp_i, i, j, g = pass_order[n]
+                if unit_pos[i] == GROUP_UNITS[grp_i] - 1 and g == 1:
+                    closing = True
+            if step == 0:
+                for slot, bank in filled:
+                    copy_slot(slot, bank, slot % 2 == 1)
+            else:
+                for k, (slot, bank) in enumerate(reversed(filled)):
+                    copy_slot(slot, bank, k == 1 if closing else k % 2 == 1)
             n_copied += len(filled)
             if step == 0:
                 quant_x(0)

from contextlib import ExitStack

import concourse.mybir as mybir
from concourse.masks import make_identity

F32 = mybir.dt.float32
BF16 = mybir.dt.bfloat16
U32 = mybir.dt.uint32
U8 = mybir.dt.uint8
FP8X4 = mybir.dt.float8_e4m3fn_x4
ALU = mybir.AluOpType
AX = mybir.AxisListType

P = 128
NODES = 64
FEAT = 1024
HID = 512
OUTF = 128
SLOTS = 4
UNITS = 16
UNIT_COLS = SLOTS * FEAT
UNIT_WORDS = UNIT_COLS // 4
PASSES = 8

FLOPS = 2 * 8192 * FEAT * HID + 2 * 128 * HID * OUTF

GROUP_UNITS = (8, 4, 2, 2)
NARROW_GROUPS = (2, 3)
HEAD_STEPS = ((16, 4),) * 6
RUN_TRANSPOSES = 16
SECOND_LAG = (16, 16, 12, 0)
TAIL_STEP = 4
SMALL_LOADS_AFTER = 6
SMALL_STEP = 10


def plan_steps():
    steps = list(HEAD_STEPS)
    transposes = sum([a for a, b in steps])
    passes = sum([b for a, b in steps])
    while transposes < UNITS * SLOTS * 4:
        a = min(RUN_TRANSPOSES, UNITS * SLOTS * 4 - transposes)
        b = a // 2
        if len(steps) == SMALL_STEP:
            a -= 4
        steps.append((a, b))
        transposes += a
        passes += b
    while passes < UNITS * PASSES:
        b = min(TAIL_STEP, UNITS * PASSES - passes)
        steps.append((0, b))
        passes += b
    return steps


def plan_passes():
    order = []
    unit0 = 0
    for grp_i, n_units in enumerate(GROUP_UNITS):
        units = range(unit0, unit0 + n_units)
        if grp_i == len(GROUP_UNITS) - 1:
            order.extend([(grp_i, i, j, g) for j in range(SLOTS) for i in units for g in range(2)])
        else:
            order.extend([(grp_i, i, j, g) for i in units for j in range(SLOTS) for g in range(2)])
        unit0 += n_units
    return order


def tile_gcn_pa_t_kernel(tc, x, W1g, b1g, W2g, b2g, out):
    nc = tc.nc
    ctx = ExitStack()
    with ctx:
        const = ctx.enter_context(tc.tile_pool(name="const", bufs=1))
        xpool = ctx.enter_context(tc.tile_pool(name="xpool", bufs=UNITS))
        gpool = ctx.enter_context(tc.tile_pool(name="gpool", bufs=3))
        cpool = ctx.enter_context(tc.tile_pool(name="cpool", bufs=5))
        epool = ctx.enter_context(tc.tile_pool(name="epool", bufs=2))
        tpool = ctx.enter_context(tc.psum_pool(name="tpool", bufs=4))
        apool = ctx.enter_context(tc.psum_pool(name="apool", bufs=1))
        ctx.enter_context(tc.manual_schedule())

        unit_group = []
        unit_pos = []
        x_views = []
        o_views = []
        x_rows = x.flatten_outer_dims()
        o_rows = out.flatten_outer_dims()
        row0 = 0
        for grp_i, n_units in enumerate(GROUP_UNITS):
            rows = n_units * SLOTS * P
            x_views.append(x_rows[row0 : row0 + rows, :].rearrange("(q s) f -> q (s f)", q=P))
            o_views.append(o_rows[row0 : row0 + rows, :].rearrange("(q s) o -> q s o", q=P))
            row0 += rows
            for c in range(n_units):
                unit_group.append(grp_i)
                unit_pos.append(c)

        ident = const.tile([P, P], F32)
        make_identity(nc, ident[:])

        xt = []
        for i in range(UNITS):
            x_sb = xpool.tile([P, UNIT_COLS], BF16, name="x_sb")
            xt.append(x_sb)
        w1raw = const.tile([P, UNIT_COLS], BF16)
        w1v = W1g.rearrange("(p j) k -> p (j k)", j=SLOTS)
        w2raw = const.tile([P, HID], BF16)
        b1raw = const.tile([P, SLOTS], BF16)
        b2raw = const.tile([P, OUTF], BF16)

        def load_x(i, pieces):
            c0 = unit_pos[i] * UNIT_COLS
            w = UNIT_COLS // pieces
            for s in range(pieces):
                nc.sync.dma_start(
                    out=xt[i][:, s * w : (s + 1) * w],
                    in_=x_views[unit_group[i]][:, c0 + s * w : c0 + (s + 1) * w],
                )

        load_x(0, SLOTS)
        for j in range(SLOTS):
            nc.sync.dma_start(out=w1raw[:, j * FEAT : (j + 1) * FEAT], in_=w1v[:, j * FEAT : (j + 1) * FEAT])
        for i in range(1, UNITS):
            load_x(i, 1)
            if i == SMALL_LOADS_AFTER:
                nc.sync.dma_start(out=w2raw[:], in_=W2g)
                nc.sync.dma_start(out=b1raw[:], in_=b1g.rearrange("(p j) -> p j", j=SLOTS))
                nc.sync.dma_start(out=b2raw[:], in_=b2g.partition_broadcast(P))

        w1grp = const.tile([P, UNIT_COLS], BF16, align_bytes=64)
        w1codes = const.tile([P, UNIT_WORDS], U32, align_bytes=64)
        w1scales = const.tile([P, UNIT_WORDS], U8, align_bytes=64)
        w2grp = const.tile([P, HID], BF16, align_bytes=64)
        w2codes = const.tile([P, OUTF], U32, align_bytes=64)
        w2scales = const.tile([P, OUTF], U8, align_bytes=64)
        b1f = const.tile([P, SLOTS], F32)
        b2f = const.tile([P, OUTF], F32)

        grouped = {}
        quantised = {}
        accs = {}
        hidden_parts = {}
        hidden_codes = {}

        def transposes(src_f32, s):
            bank = tpool.tile([P, 512], F32, name="bank")
            for v in range(4):
                nc.tensor.transpose(
                    bank[:, v * P : (v + 1) * P],
                    src_f32[:, s * 512 + v * P : s * 512 + (v + 1) * P],
                    ident[:],
                )
            return bank

        def copy_slot(slot, bank, on_vector):
            i, s = divmod(slot, SLOTS)
            if i not in grouped:
                grp = gpool.tile([P, UNIT_COLS], BF16, name="grp", align_bytes=64)
                grouped[i] = grp
            dst = grouped[i][:].bitcast(F32).rearrange("p (g h q u) -> p g h q u", g=2, h=SLOTS, q=P, u=2)
            src = bank[:].rearrange("p (g u q) -> p g q u", g=2, u=2, q=P)
            if on_vector:
                nc.vector.tensor_copy(out=dst[:, :, s, :, :], in_=src)
            else:
                nc.scalar.copy(out=dst[:, :, s, :, :], in_=src)

        def quant_x(i):
            codes = cpool.tile([P, UNIT_WORDS], U32, name="codes", align_bytes=64)
            scales = cpool.tile([P, UNIT_WORDS], U8, name="scales", align_bytes=64)
            nc.vector.quantize_mx(out=codes[:].bitcast(FP8X4), scales=scales[:], in_=grouped[i][:])
            quantised[i] = (codes, scales)

        def prep_w1():
            src = w1raw[:].bitcast(F32)
            grp_v = w1grp[:].bitcast(F32).rearrange("p (j g m u) -> p j g m u", j=SLOTS, g=2, m=P, u=2)
            for j in range(SLOTS):
                bank = transposes(src, j)
                nc.scalar.copy(out=grp_v[:, j, :, :, :], in_=bank[:].rearrange("p (g u m) -> p g m u", g=2, u=2, m=P))
                nc.vector.quantize_mx(
                    out=w1codes[:, j * 256 : (j + 1) * 256].bitcast(FP8X4),
                    scales=w1scales[:, j * 256 : (j + 1) * 256],
                    in_=w1grp[:, j * FEAT : (j + 1) * FEAT],
                )

        def prep_small():
            src = w2raw[:].bitcast(F32).rearrange("p (w u) -> p u w", u=2)
            bank = tpool.tile([P, 512], F32, name="bank")
            for u in range(2):
                nc.tensor.transpose(bank[:, u * P : (u + 1) * P], src[:, u, :], ident[:])
            nc.vector.tensor_copy(
                out=w2grp[:].bitcast(F32).rearrange("p (o u) -> p o u", u=2),
                in_=bank[:, 0 : 2 * P].rearrange("p (u o) -> p o u", u=2),
            )
            nc.vector.tensor_copy(out=b1f[:], in_=b1raw[:])
            nc.vector.tensor_copy(out=b2f[:], in_=b2raw[:])
            nc.vector.quantize_mx(out=w2codes[:].bitcast(FP8X4), scales=w2scales[:], in_=w2grp[:])

        def one_pass(grp_i, i, j, g):
            first = unit_pos[i] == 0 and g == 0
            last = unit_pos[i] == GROUP_UNITS[grp_i] - 1 and g == 1
            if first:
                acc = apool.tile([P, 512], F32, name="acc%d" % j)
                accs[j] = acc
            codes, scales = quantised[i]
            w = (j * 2 + g) * P
            parts = 2 if grp_i in NARROW_GROUPS else 1
            width = 512 // parts
            for part in range(parts):
                c0 = g * 512 + part * width
                nc.tensor.matmul_mx(
                    out=accs[j][:, 0:width],
                    lhsT=w1codes[:, w : w + P].bitcast(FP8X4),
                    lhsT_scale=w1scales[:, w : w + P],
                    rhs=codes[:, c0 : c0 + width].bitcast(FP8X4),
                    rhs_scale=scales[:, c0 : c0 + width],
                    start=(first and part == 0),
                    stop=(last and part == parts - 1),
                )
            return last

        def node_sum(grp_i, j):
            nb = 8 * GROUP_UNITS[grp_i]
            parts = 2 if grp_i in NARROW_GROUPS else 1
            if j == 0:
                sums = epool.tile([P, 256], F32, name="sums")
                m1pre = epool.tile([P, HID], BF16, name="m1pre")
                hidden_parts[grp_i] = (sums, m1pre)
            sums, m1pre = hidden_parts[grp_i]
            nc.vector.tensor_reduce(
                out=sums[:, j * nb : (j + 1) * nb],
                in_=accs[j][:, 0 : 512 // parts].rearrange("p (h b l) -> p b h l", h=SLOTS // parts, b=nb, l=P // nb),
                axis=AX.XY,
                op=ALU.add,
            )
            nc.vector.tensor_scalar(
                out=m1pre[:].rearrange("p (b r j) -> p b r j", b=nb, r=P // nb, j=SLOTS)[:, :, :, j],
                in0=sums[:, j * nb : (j + 1) * nb].unsqueeze(2).to_broadcast([P, nb, P // nb]),
                scalar1=1.0 / NODES,
                scalar2=b1f[:, j : j + 1],
                op0=ALU.mult,
                op1=ALU.add,
            )

        def hidden(grp_i):
            m1pre = hidden_parts[grp_i][1]
            m1 = epool.tile([P, HID], BF16, name="m1", align_bytes=64)
            nc.vector.tensor_scalar_max(out=m1[:], in0=m1pre[:], scalar1=0.0)
            m1codes = epool.tile([P, P], U32, name="m1codes", align_bytes=64)
            m1scales = epool.tile([P, P], U8, name="m1scales", align_bytes=64)
            nc.vector.quantize_mx(out=m1codes[:].bitcast(FP8X4), scales=m1scales[:], in_=m1[:])
            hidden_codes[grp_i] = (m1codes, m1scales)

        def second(grp_i):
            m1codes, m1scales = hidden_codes[grp_i]
            bank = tpool.tile([P, 512], F32, name="bank")
            nc.tensor.matmul_mx(
                out=bank[:, 0:OUTF],
                lhsT=m1codes[:].bitcast(FP8X4),
                lhsT_scale=m1scales[:],
                rhs=w2codes[:].bitcast(FP8X4),
                rhs_scale=w2scales[:],
                start=True,
                stop=True,
            )
            pre2 = epool.tile([P, OUTF], F32, name="pre2")
            nc.vector.tensor_tensor(out=pre2[:], in0=bank[:, 0:OUTF], in1=b2f[:], op=ALU.add)
            m2 = epool.tile([P, OUTF], F32, name="m2")
            nc.vector.tensor_scalar_max(out=m2[:], in0=pre2[:], scalar1=0.0)
            n_rep = SLOTS * GROUP_UNITS[grp_i]
            nc.sync.dma_start(out=o_views[grp_i], in_=m2[:].unsqueeze(1).to_broadcast([P, n_rep, OUTF]))

        pass_order = plan_passes()
        n_transposes = 0
        n_copied = 0
        n_passes = 0
        n_quant = 0
        to_hide = []
        to_second = []
        open_bank = None
        for step, (run_transposes, run_passes) in enumerate(plan_steps()):
            while n_quant < UNITS and SLOTS * (n_quant + 1) <= n_copied:
                quant_x(n_quant)
                n_quant += 1
            for grp_i in to_hide:
                hidden(grp_i)
            to_hide = []
            filled = []
            for k in range(run_transposes):
                slot, v = divmod(n_transposes, 4)
                i, s = divmod(slot, SLOTS)
                if v == 0:
                    open_bank = tpool.tile([P, 512], F32, name="bank")
                nc.tensor.transpose(
                    open_bank[:, v * P : (v + 1) * P],
                    xt[i][:].bitcast(F32)[:, s * 512 + v * P : s * 512 + (v + 1) * P],
                    ident[:],
                )
                if v == 3:
                    filled.append((slot, open_bank))
                n_transposes += 1
            closing = False
            for n in range(n_passes, min(n_passes + run_passes, UNITS * PASSES)):
                grp_i, i, j, g = pass_order[n]
                if unit_pos[i] == GROUP_UNITS[grp_i] - 1 and g == 1:
                    closing = True
            if step == 0:
                for slot, bank in filled:
                    copy_slot(slot, bank, slot % 2 == 1)
            else:
                for k, (slot, bank) in enumerate(reversed(filled)):
                    copy_slot(slot, bank, k == 1 if closing else k % 2 == 1)
            n_copied += len(filled)
            if step == 0:
                quant_x(0)
                n_quant = 1
                prep_w1()
            if step == SMALL_STEP:
                prep_small()
            for k in range(run_passes):
                grp_i, i, j, g = pass_order[n_passes]
                closes = one_pass(grp_i, i, j, g)
                n_passes += 1
                if closes:
                    node_sum(grp_i, j)
                    if j == SLOTS - 1:
                        to_hide.append(grp_i)
                        to_second.append((grp_i, n_passes))
            if n_passes == UNITS * PASSES:
                for grp_i in to_hide:
                    hidden(grp_i)
                to_hide = []
            while to_second and (
                n_passes - to_second[0][1] >= SECOND_LAG[to_second[0][0]] or n_passes == UNITS * PASSES
            ):
                second(to_second[0][0])
                to_second = to_second[1:]
